import numpy as np
import ml_dtypes


def mxq(x, axis, fmt="e4m3"):
    dtype, down = {"e4m3": (ml_dtypes.float8_e4m3fn, 7), "e5m2": (ml_dtypes.float8_e5m2, 14)}[fmt]
    v = np.moveaxis(np.asarray(x, np.float32).astype(ml_dtypes.bfloat16).astype(np.float64), axis, -1)
    blocks = v.reshape(v.shape[:-1] + (-1, 32))
    amax = np.abs(blocks).max(-1, keepdims=True)
    byte = np.maximum(np.where(amax > 0, np.frexp(amax)[1] - 1 + 127, 0) - down, 1)
    scale = np.exp2(byte - 127.0)
    codes = (blocks / scale).astype(np.float32).astype(dtype).astype(np.float64)
    return np.moveaxis((codes * scale).reshape(v.shape), -1, axis)


WIDE = False


def mx_kscale(k):
    if not WIDE:
        return np.ones(k)
    levels = np.array([10, -10, 5, -5, 0])
    a = np.random.permutation(np.resize(levels, k // 512 * 4)).reshape(k // 512, 4)
    idx = np.arange(k)
    return np.exp2(a[idx // 512, idx % 128 // 32])


BF16 = ml_dtypes.bfloat16


def bf(x):
    return np.asarray(x, np.float32).astype(BF16)


def f64(x):
    return np.asarray(x).astype(np.float64)


B, IN, H, Z, G = 8192, 512, 128, 128, 4


def setup_inputs():
    s = mx_kscale(IN)
    return {"src_x": bf(np.random.standard_normal((B, IN)) * s),
            "zx": bf(np.random.standard_normal((B, G, Z))),
            "dx_w": bf(np.random.standard_normal((G, H, Z)) / np.sqrt(Z)),
            "w_x": bf(np.random.standard_normal((G, H, IN)) / np.sqrt(IN) / s)}


def reference(src_x, zx, dx_w, w_x):
    d_x = (f64(zx).transpose(1, 0, 2) @ f64(dx_w).transpose(0, 2, 1)).transpose(1, 0, 2)
    wx = (mxq(f64(src_x), 1, "e4m3") @ mxq(f64(w_x).reshape(G * H, IN), 1, "e4m3").T).reshape(B, G, H)
    return d_x * wx

@@ -1,0 +1,183 @@
+from contextlib import ExitStack
+
+import concourse.mybir as mybir
+from concourse.masks import make_identity
+
+BF16 = mybir.dt.bfloat16
+F32 = mybir.dt.float32
+U32 = mybir.dt.uint32
+U8 = mybir.dt.uint8
+FP8X4 = mybir.dt.float8_e4m3fn_x4
+MULT = mybir.AluOpType.mult
+
+P = 128
+B, IN, H, Z, G = 8192, 512, 128, 128, 4
+FLOPS = 2 * B * IN * G * H + 2 * B * G * H * Z
+ROW = 512
+NT = B // P
+GT = 2
+NG = NT // GT
+CH = 8
+NCH = NT // CH
+ST = 4
+EARLY = 5
+LATE_AFTER_STORE = {1: 5, 3: 6, 5: 7}
+STORES = [(s, s + ST) for s in range(0, NT - ST, ST)] + [(NT - 4, NT - 2), (NT - 2, NT - 1), (NT - 1, NT)]
+
+
+def tile_metalstmcell_pa_t_kernel(tc, src_x, zx, dx_w, w_x, out):
+    nc = tc.nc
+    x_v = src_x.rearrange("(p t) k -> p (t k)", t=NT)
+    z_v = zx.rearrange("(p t) g z -> p (t g z)", t=NT)
+    o_v = out.rearrange("(p t) g h -> p (t g h)", t=NT)
+
+    with ExitStack() as ctx:
+        const = ctx.enter_context(tc.tile_pool(name="const", bufs=1))
+        xin = ctx.enter_context(tc.tile_pool(name="xin", bufs=1))
+        work = ctx.enter_context(tc.tile_pool(name="work", bufs=3))
+        outp = ctx.enter_context(tc.tile_pool(name="outp", bufs=7))
+        ps = ctx.enter_context(tc.psum_pool(name="ps", bufs=2))
+        ctx.enter_context(tc.manual_schedule())
+
+        ident_f = const.tile([P, P], F32, name="ident_f")
+        make_identity(nc, ident_f[:])
+        ident_b = const.tile([P, P], BF16, name="ident_b")
+        make_identity(nc, ident_b[:])
+
+        x_sb = []
+        z_sb = []
+        for c in range(NCH):
+            x_sb.append(xin.tile([P, CH * ROW], BF16, name="x%d" % c))
+            z_sb.append(xin.tile([P, CH * ROW], BF16, name="z%d" % c))
+
+        def load(c, t0, t1):
+            lo = t0 * ROW
+            hi = t1 * ROW
+            base = c * CH * ROW
+            nc.sync.dma_start(out=x_sb[c][:, lo:hi], in_=x_v[:, base + lo:base + hi])
+            nc.sync.dma_start(out=z_sb[c][:, lo:hi], in_=z_v[:, base + lo:base + hi])
+
+        w_sb = const.tile([P, G * IN], BF16, name="w_sb")
+        dw_sb = const.tile([P, G * Z], BF16, name="dw_sb")
+        load(0, 0, GT)
+        nc.sync.dma_start(out=w_sb[:].rearrange("h (g k) -> h g k", g=G), in_=w_x.rearrange("g h k -> h g k"))
+        nc.sync.dma_start(out=dw_sb[:].rearrange("h (g z) -> h g z", g=G), in_=dx_w.rearrange("g h z -> h g z"))
+        load(0, GT, CH)
+        for c in range(1, EARLY):
+            load(c, 0, CH)
+
+        banks = {}
+        ready = {}
+        codes = {}
+
+        def transposes(j):
+            xp = ps.tile([P, GT, 2, P], F32, name="xp", tag="xp")
+            zp = ps.tile([P, GT, G, P], BF16, name="zp", tag="zp")
+            for a in range(GT):
+                c, tl = divmod(j * GT + a, CH)
+                xw = x_sb[c][:].bitcast(F32)
+                for u in range(2):
+                    lo = tl * (ROW // 2) + u * P
+                    nc.tensor.transpose(xp[:, a, u, :], xw[:, lo:lo + P], ident_f[:])
+            for a in range(GT):
+                c, tl = divmod(j * GT + a, CH)
+                for g in range(G):
+                    lo = tl * ROW + g * Z
+                    nc.tensor.transpose(zp[:, a, g, :], z_sb[c][:, lo:lo + Z], ident_b[:])
+            banks[j] = (xp, zp)
+
+        def evacuate(j, x_on_scalar):
+            xp, zp = banks[j]
+            xg = work.tile([P, GT * P * 4], BF16, name="xg", tag="xg", align_bytes=64)
+            dst = xg[:].bitcast(F32).rearrange("p (a b u) -> p a b u", a=GT, u=2)
+            src = xp[:].rearrange("p a u b -> p a b u")
+            if x_on_scalar:
+                nc.scalar.copy(out=dst, in_=src)
+            else:
+                nc.vector.tensor_copy(out=dst, in_=src)
+            zt = work.tile([P, GT * G * P], BF16, name="zt", tag="zt", bufs=4)
+            nc.scalar.copy(out=zt[:], in_=zp[:].rearrange("p a g b -> p (a g b)"))
+            ready[j] = (xg, zt)
+
+        def quantise(j):
+            xg = ready[j][0]
+            xc = work.tile([P, GT * P], U32, name="xc", tag="xc", align_bytes=64)
+            xs = work.tile([P, GT * P], U8, name="xs", tag="xs", align_bytes=64)
+            nc.vector.quantize_mx(out=xc[:].bitcast(FP8X4), scales=xs[:], in_=xg[:])
+            codes[j] = (xc, xs)
+
+        transposes(0)
+        evacuate(0, False)
+
+        wg = const.tile([P, G * H * 4], BF16, name="wg", align_bytes=64)
+        wgf = wg[:].bitcast(F32).rearrange("p (q a n u) -> p q a n u", q=2, a=GT, u=2)
+        wf = w_sb[:].bitcast(F32)
+        for q in range(2):
+            wt = ps.tile([P, GT, 2, P], F32, name="xp", tag="xp")
+            for a in range(GT):
+                for u in range(2):
+                    lo = (q * GT + a) * (IN // 2) + u * P
+                    nc.tensor.transpose(wt[:, a, u, :], wf[:, lo:lo + P], ident_f[:])
+            if q == 0:
+                nc.scalar.copy(out=wgf[:, q], in_=wt[:].rearrange("p a u n -> p a n u"))
+            else:
+                nc.vector.tensor_copy(out=wgf[:, q], in_=wt[:].rearrange("p a u n -> p a n u"))
+        dwp = ps.tile([P, GT, G, P], BF16, name="zp", tag="zp")
+        for g in range(G):
+            nc.tensor.transpose(dwp[:, 0, g, :], dw_sb[:, g * Z:(g + 1) * Z], ident_b[:])
+        dwt = const.tile([P, G * H], BF16, name="dwt")
+        nc.scalar.copy(out=dwt[:], in_=dwp[:, 0].rearrange("p g h -> p (g h)"))
+        quantise(0)
+        wc = const.tile([P, G * H], U32, name="wc", align_bytes=64)
+        ws = const.tile([P, G * H], U8, name="ws", align_bytes=64)
+        nc.vector.quantize_mx(out=wc[:].bitcast(FP8X4), scales=ws[:], in_=wg[:])
+
+        transposes(1)
+        evacuate(1, False)
+
+        obs = {}
+        n_stored = 0
+        for j in range(NG):
+            if j + 2 < NG:
+                transposes(j + 2)
+                evacuate(j + 2, j % 2 == 0)
+            if j + 1 < NG:
+                quantise(j + 1)
+            zt = ready[j][1]
+            xc, xs = codes[j]
+            dps = []
+            for a in range(GT):
+                dp = ps.tile([P, ROW], F32, name="dp", tag="dp")
+                for g in range(G):
+                    lo = (a * G + g) * P
+                    nc.tensor.matmul(dp[:, g * H:(g + 1) * H], lhsT=zt[:, lo:lo + P],
+                                     rhs=dwt[:, g * H:(g + 1) * H], start=True, stop=True)
+                dps.append(dp)
+            wps = []
+            for a in range(GT):
+                wp = ps.tile([P, ROW], F32, name="wp", tag="wp")
+                nc.tensor.matmul_mx(out=wp[:], lhsT=xc[:, a * P:(a + 1) * P].bitcast(FP8X4),
+                                    lhsT_scale=xs[:, a * P:(a + 1) * P],
+                                    rhs=wc[:].bitcast(FP8X4), rhs_scale=ws[:], start=True, stop=True)
+                wps.append(wp)
+            dss = []
+            for a in range(GT):
+                ds = work.tile([P, ROW], F32, name="ds", tag="ds", bufs=4)
+                nc.scalar.copy(out=ds[:], in_=dps[a][:])
+                dss.append(ds)
+            for a in range(GT):
+                t = j * GT + a
+                slot, tl = divmod(t, ST)
+                if tl == 0:
+                    ob = outp.tile([P, ST * ROW], F32, name="ob", tag="ob")
+                    obs[slot] = ob
+                nc.vector.tensor_tensor(out=obs[slot][:, tl * ROW:(tl + 1) * ROW], in0=wps[a][:],
+                                        in1=dss[a][:], op=MULT)
+                s0, s1 = STORES[n_stored]
+                if t + 1 == s1:
+                    nc.sync.dma_start(out=o_v[:, s0 * ROW:s1 * ROW],
+                                      in_=obs[slot][:, (s0 - slot * ST) * ROW:(s1 - slot * ST) * ROW])
+                    late = LATE_AFTER_STORE.get(n_stored)
+                    if late is not None:
+                        load(late, 0, CH)
+                    n_stored += 1

@@ -59,16 +59,18 @@ def tile_metalstmcell_pa_t_kernel(tc, src_x, zx, dx_w, w_x, out):
 
         w_sb = const.tile([P, G * IN], BF16, name="w_sb")
         dw_sb = const.tile([P, G * Z], BF16, name="dw_sb")
-        load(0, 0, GT)
-        nc.sync.dma_start(out=w_sb[:].rearrange("h (g k) -> h g k", g=G), in_=w_x.rearrange("g h k -> h g k"))
+        load(0, 0, 2)
+        load(0, 2, 4)
         nc.sync.dma_start(out=dw_sb[:].rearrange("h (g z) -> h g z", g=G), in_=dx_w.rearrange("g h z -> h g z"))
-        load(0, GT, CH)
+        nc.sync.dma_start(out=w_sb[:].rearrange("h (g k) -> h g k", g=G), in_=w_x.rearrange("g h k -> h g k"))
+        load(0, 4, CH)
         for c in range(1, EARLY):
             load(c, 0, CH)
 
         banks = {}
         ready = {}
         codes = {}
+        dcopy = {}
 
         def transposes(j):
             xp = ps.tile([P, GT, 2, P], F32, name="xp", tag="xp")
@@ -95,7 +97,7 @@ def tile_metalstmcell_pa_t_kernel(tc, src_x, zx, dx_w, w_x, out):
                 nc.scalar.copy(out=dst, in_=src)
             else:
                 nc.vector.tensor_copy(out=dst, in_=src)
-            zt = work.tile([P, GT * G * P], BF16, name="zt", tag="zt", bufs=4)
+            zt = work.tile([P, GT * G * P], BF16, name="zt", tag="zt")
             nc.scalar.copy(out=zt[:], in_=zp[:].rearrange("p a g b -> p (a g b)"))
             ready[j] = (xg, zt)
 
@@ -106,8 +108,32 @@ def tile_metalstmcell_pa_t_kernel(tc, src_x, zx, dx_w, w_x, out):
             nc.vector.quantize_mx(out=xc[:].bitcast(FP8X4), scales=xs[:], in_=xg[:])
             codes[j] = (xc, xs)
 
+        def scalings(j):
+            zt = ready[j][1]
+            dps = []
+            for a in range(GT):
+                dp = ps.tile([P, ROW], F32, name="dp", tag="dp")
+                for g in range(G):
+                    lo = (a * G + g) * P
+                    nc.tensor.matmul(dp[:, g * H:(g + 1) * H], lhsT=zt[:, lo:lo + P],
+                                     rhs=dwt[:, g * H:(g + 1) * H], start=True, stop=True)
+                dps.append(dp)
+            dss = []
+            for a in range(GT):
+                ds = work.tile([P, ROW], F32, name="ds", tag="ds", bufs=6)
+                nc.scalar.copy(out=ds[:], in_=dps[a][:])
+                dss.append(ds)
+            dcopy[j] = dss
+
         transposes(0)
+        transposes(1)
         evacuate(0, False)
+        dwp = ps.tile([P, GT, G, P], BF16, name="zp", tag="zp")
+        for g in range(G):
+            nc.tensor.transpose(dwp[:, 0, g, :], dw_sb[:, g * Z:(g + 1) * Z], ident_b[:])
+        dwt = const.tile([P, G * H], BF16, name="dwt")
+        nc.scalar.copy(out=dwt[:], in_=dwp[:, 0].rearrange("p g h -> p (g h)"))
+        evacuate(1, False)
 
         wg = const.tile([P, G * H * 4], BF16, name="wg", align_bytes=64)
         wgf = wg[:].bitcast(F32).rearrange("p (q a n u) -> p q a n u", q=2, a=GT, u=2)
@@ -122,37 +148,24 @@ def tile_metalstmcell_pa_t_kernel(tc, src_x, zx, dx_w, w_x, out):
                 nc.scalar.copy(out=wgf[:, q], in_=wt[:].rearrange("p a u n -> p a n u"))
             else:
                 nc.vector.tensor_copy(out=wgf[:, q], in_=wt[:].rearrange("p a u n -> p a n u"))
-        dwp = ps.tile([P, GT, G, P], BF16, name="zp", tag="zp")
-        for g in range(G):
-            nc.tensor.transpose(dwp[:, 0, g, :], dw_sb[:, g * Z:(g + 1) * Z], ident_b[:])
-        dwt = const.tile([P, G * H], BF16, name="dwt")
-        nc.scalar.copy(out=dwt[:], in_=dwp[:, 0].rearrange("p g h -> p (g h)"))
         quantise(0)
         wc = const.tile([P, G * H], U32, name="wc", align_bytes=64)
         ws = const.tile([P, G * H], U8, name="ws", align_bytes=64)
         nc.vector.quantize_mx(out=wc[:].bitcast(FP8X4), scales=ws[:], in_=wg[:])
-
-        transposes(1)
-        evacuate(1, False)
+        transposes(2)
+        scalings(0)
 
         obs = {}
         n_stored = 0
         for j in range(NG):
+            if j + 3 < NG:
+                transposes(j + 3)
             if j + 2 < NG:
-                transposes(j + 2)
                 evacuate(j + 2, j % 2 == 0)
             if j + 1 < NG:
                 quantise(j + 1)
-            zt = ready[j][1]
+                scalings(j + 1)
             xc, xs = codes[j]
-            dps = []
-            for a in range(GT):
-                dp = ps.tile([P, ROW], F32, name="dp", tag="dp")
-                for g in range(G):
-                    lo = (a * G + g) * P
-                    nc.tensor.matmul(dp[:, g * H:(g + 1) * H], lhsT=zt[:, lo:lo + P],
-                                     rhs=dwt[:, g * H:(g + 1) * H], start=True, stop=True)
-                dps.append(dp)
             wps = []
             for a in range(GT):
                 wp = ps.tile([P, ROW], F32, name="wp", tag="wp")
@@ -160,11 +173,6 @@ def tile_metalstmcell_pa_t_kernel(tc, src_x, zx, dx_w, w_x, out):
                                     lhsT_scale=xs[:, a * P:(a + 1) * P],
                                     rhs=wc[:].bitcast(FP8X4), rhs_scale=ws[:], start=True, stop=True)
                 wps.append(wp)
-            dss = []
-            for a in range(GT):
-                ds = work.tile([P, ROW], F32, name="ds", tag="ds", bufs=4)
-                nc.scalar.copy(out=ds[:], in_=dps[a][:])
-                dss.append(ds)
             for a in range(GT):
                 t = j * GT + a
                 slot, tl = divmod(t, ST)
@@ -172,7 +180,7 @@ def tile_metalstmcell_pa_t_kernel(tc, src_x, zx, dx_w, w_x, out):
                     ob = outp.tile([P, ST * ROW], F32, name="ob", tag="ob")
                     obs[slot] = ob
                 nc.vector.tensor_tensor(out=obs[slot][:, tl * ROW:(tl + 1) * ROW], in0=wps[a][:],
-                                        in1=dss[a][:], op=MULT)
+                                        in1=dcopy[j][a][:], op=MULT)
                 s0, s1 = STORES[n_stored]
                 if t + 1 == s1:
                     nc.sync.dma_start(out=o_v[:, s0 * ROW:s1 * ROW],

@@ -74,7 +74,7 @@ def tile_metalstmcell_pa_t_kernel(tc, src_x, zx, dx_w, w_x, out):
 
         def transposes(j):
             xp = ps.tile([P, GT, 2, P], F32, name="xp", tag="xp")
-            zp = ps.tile([P, GT, G, P], BF16, name="zp", tag="zp")
+            zp = ps.tile([P, GT * G * P], BF16, name="zp", tag="zp")
             for a in range(GT):
                 c, tl = divmod(j * GT + a, CH)
                 xw = x_sb[c][:].bitcast(F32)
@@ -85,7 +85,7 @@ def tile_metalstmcell_pa_t_kernel(tc, src_x, zx, dx_w, w_x, out):
                 c, tl = divmod(j * GT + a, CH)
                 for g in range(G):
                     lo = tl * ROW + g * Z
-                    nc.tensor.transpose(zp[:, a, g, :], z_sb[c][:, lo:lo + Z], ident_b[:])
+                    nc.tensor.transpose(zp[:, (a * G + g) * P:(a * G + g + 1) * P], z_sb[c][:, lo:lo + Z], ident_b[:])
             banks[j] = (xp, zp)
 
         def evacuate(j, x_on_scalar):
@@ -98,7 +98,7 @@ def tile_metalstmcell_pa_t_kernel(tc, src_x, zx, dx_w, w_x, out):
             else:
                 nc.vector.tensor_copy(out=dst, in_=src)
             zt = work.tile([P, GT * G * P], BF16, name="zt", tag="zt")
-            nc.scalar.copy(out=zt[:], in_=zp[:].rearrange("p a g b -> p (a g b)"))
+            nc.scalar.copy(out=zt[:].bitcast(F32), in_=zp[:].bitcast(F32))
             ready[j] = (xg, zt)
 
         def quantise(j):
@@ -128,11 +128,11 @@ def tile_metalstmcell_pa_t_kernel(tc, src_x, zx, dx_w, w_x, out):
         transposes(0)
         transposes(1)
         evacuate(0, False)
-        dwp = ps.tile([P, GT, G, P], BF16, name="zp", tag="zp")
+        dwp = ps.tile([P, GT * G * P], BF16, name="zp", tag="zp")
         for g in range(G):
-            nc.tensor.transpose(dwp[:, 0, g, :], dw_sb[:, g * Z:(g + 1) * Z], ident_b[:])
+            nc.tensor.transpose(dwp[:, g * H:(g + 1) * H], dw_sb[:, g * Z:(g + 1) * Z], ident_b[:])
         dwt = const.tile([P, G * H], BF16, name="dwt")
-        nc.scalar.copy(out=dwt[:], in_=dwp[:, 0].rearrange("p g h -> p (g h)"))
+        nc.scalar.copy(out=dwt[:].bitcast(F32), in_=dwp[:, 0:G * H].bitcast(F32))
         evacuate(1, False)
 
         wg = const.tile([P, G * H * 4], BF16, name="wg", align_bytes=64)

@@ -71,6 +71,7 @@ def tile_metalstmcell_pa_t_kernel(tc, src_x, zx, dx_w, w_x, out):
         ready = {}
         codes = {}
         dcopy = {}
+        dbank = {}
 
         def transposes(j):
             xp = ps.tile([P, GT, 2, P], F32, name="xp", tag="xp")
@@ -108,20 +109,20 @@ def tile_metalstmcell_pa_t_kernel(tc, src_x, zx, dx_w, w_x, out):
             nc.vector.quantize_mx(out=xc[:].bitcast(FP8X4), scales=xs[:], in_=xg[:])
             codes[j] = (xc, xs)
 
-        def scalings(j):
+        def scaling_matmuls(j, a):
             zt = ready[j][1]
-            dps = []
-            for a in range(GT):
-                dp = ps.tile([P, ROW], F32, name="dp", tag="dp")
-                for g in range(G):
-                    lo = (a * G + g) * P
-                    nc.tensor.matmul(dp[:, g * H:(g + 1) * H], lhsT=zt[:, lo:lo + P],
-                                     rhs=dwt[:, g * H:(g + 1) * H], start=True, stop=True)
-                dps.append(dp)
+            dp = ps.tile([P, ROW], F32, name="dp", tag="dp")
+            for g in range(G):
+                lo = (a * G + g) * P
+                nc.tensor.matmul(dp[:, g * H:(g + 1) * H], lhsT=zt[:, lo:lo + P],
+                                 rhs=dwt[:, g * H:(g + 1) * H], start=True, stop=True)
+            dbank[(j, a)] = dp
+
+        def scaling_copies(j):
             dss = []
             for a in range(GT):
                 ds = work.tile([P, ROW], F32, name="ds", tag="ds", bufs=6)
-                nc.scalar.copy(out=ds[:], in_=dps[a][:])
+                nc.scalar.copy(out=ds[:], in_=dbank[(j, a)][:])
                 dss.append(ds)
             dcopy[j] = dss
 
@@ -153,7 +154,9 @@ def tile_metalstmcell_pa_t_kernel(tc, src_x, zx, dx_w, w_x, out):
         ws = const.tile([P, G * H], U8, name="ws", align_bytes=64)
         nc.vector.quantize_mx(out=wc[:].bitcast(FP8X4), scales=ws[:], in_=wg[:])
         transposes(2)
-        scalings(0)
+        scaling_matmuls(0, 0)
+        scaling_matmuls(0, 1)
+        scaling_copies(0)
 
         obs = {}
         n_stored = 0
@@ -164,7 +167,7 @@ def tile_metalstmcell_pa_t_kernel(tc, src_x, zx, dx_w, w_x, out):
                 evacuate(j + 2, j % 2 == 0)
             if j + 1 < NG:
                 quantise(j + 1)
-                scalings(j + 1)
+                scaling_matmuls(j + 1, 0)
             xc, xs = codes[j]
             wps = []
             for a in range(GT):
@@ -173,6 +176,9 @@ def tile_metalstmcell_pa_t_kernel(tc, src_x, zx, dx_w, w_x, out):
                                     lhsT_scale=xs[:, a * P:(a + 1) * P],
                                     rhs=wc[:].bitcast(FP8X4), rhs_scale=ws[:], start=True, stop=True)
                 wps.append(wp)
+            if j + 1 < NG:
+                scaling_matmuls(j + 1, 1)
+                scaling_copies(j + 1)
             for a in range(GT):
                 t = j * GT + a
                 slot, tl = divmod(t, ST)

@@ -17,12 +17,13 @@ ROW = 512
 NT = B // P
 GT = 2
 NG = NT // GT
-CH = 8
-NCH = NT // CH
-ST = 4
-EARLY = 5
-LATE_AFTER_STORE = {1: 5, 3: 6, 5: 7}
-STORES = [(s, s + ST) for s in range(0, NT - ST, ST)] + [(NT - 4, NT - 2), (NT - 2, NT - 1), (NT - 1, NT)]
+CHUNKS = [(0, 16), (16, 24), (24, 32), (32, 48), (48, 64)]
+CHUNK_TAG = ["a", "b", "c", "d", "a"]
+EARLY_LOADS = [(2, 4), (4, 6), (6, 8), (8, 12), (12, 16), (16, 24), (24, 32), (32, 48)]
+LATE_LOADS = {1: [(48, 64)]}
+ST = 8
+STORE_SIZES = [8, 8, 8, 8, 8, 4, 4, 4, 4, 2, 2, 2, 1, 1]
+DUMMIES = [0, 0, 0, 0, 0]
 
 
 def tile_metalstmcell_pa_t_kernel(tc, src_x, zx, dx_w, w_x, out):
@@ -35,37 +36,44 @@ def tile_metalstmcell_pa_t_kernel(tc, src_x, zx, dx_w, w_x, out):
         const = ctx.enter_context(tc.tile_pool(name="const", bufs=1))
         xin = ctx.enter_context(tc.tile_pool(name="xin", bufs=1))
         work = ctx.enter_context(tc.tile_pool(name="work", bufs=3))
-        outp = ctx.enter_context(tc.tile_pool(name="outp", bufs=7))
+        outp = ctx.enter_context(tc.tile_pool(name="outp", bufs=4))
         ps = ctx.enter_context(tc.psum_pool(name="ps", bufs=2))
         ctx.enter_context(tc.manual_schedule())
 
-        ident_f = const.tile([P, P], F32, name="ident_f")
-        make_identity(nc, ident_f[:])
+        def dummies(n):
+            assert n == 0
+
         ident_b = const.tile([P, P], BF16, name="ident_b")
         make_identity(nc, ident_b[:])
+        ident_f = const.tile([P, P], F32, name="ident_f")
+        make_identity(nc, ident_f[:])
 
-        x_sb = []
-        z_sb = []
-        for c in range(NCH):
-            x_sb.append(xin.tile([P, CH * ROW], BF16, name="x%d" % c))
-            z_sb.append(xin.tile([P, CH * ROW], BF16, name="z%d" % c))
+        x_sb = {}
+        z_sb = {}
 
-        def load(c, t0, t1):
-            lo = t0 * ROW
-            hi = t1 * ROW
-            base = c * CH * ROW
-            nc.sync.dma_start(out=x_sb[c][:, lo:hi], in_=x_v[:, base + lo:base + hi])
-            nc.sync.dma_start(out=z_sb[c][:, lo:hi], in_=z_v[:, base + lo:base + hi])
+        def chunk_of(t):
+            for c in range(len(CHUNKS)):
+                if CHUNKS[c][0] <= t < CHUNKS[c][1]:
+                    return c, t - CHUNKS[c][0]
+            raise ValueError("no chunk")
+
+        def load(t0, t1):
+            c, lo = chunk_of(t0)
+            n = CHUNKS[c][1] - CHUNKS[c][0]
+            if c not in x_sb:
+                x_sb[c] = xin.tile([P, n * ROW], BF16, name="x%s" % CHUNK_TAG[c], tag="x%s" % CHUNK_TAG[c])
+                z_sb[c] = xin.tile([P, n * ROW], BF16, name="z%s" % CHUNK_TAG[c], tag="z%s" % CHUNK_TAG[c])
+            hi = lo + t1 - t0
+            nc.sync.dma_start(out=x_sb[c][:, lo * ROW:hi * ROW], in_=x_v[:, t0 * ROW:t1 * ROW])
+            nc.sync.dma_start(out=z_sb[c][:, lo * ROW:hi * ROW], in_=z_v[:, t0 * ROW:t1 * ROW])
 
         w_sb = const.tile([P, G * IN], BF16, name="w_sb")
         dw_sb = const.tile([P, G * Z], BF16, name="dw_sb")
-        load(0, 0, 2)
-        load(0, 2, 4)
         nc.sync.dma_start(out=dw_sb[:].rearrange("h (g z) -> h g z", g=G), in_=dx_w.rearrange("g h z -> h g z"))
+        load(0, 2)
         nc.sync.dma_start(out=w_sb[:].rearrange("h (g k) -> h g k", g=G), in_=w_x.rearrange("g h k -> h g k"))
-        load(0, 4, CH)
-        for c in range(1, EARLY):
-            load(c, 0, CH)
+        for t0, t1 in EARLY_LOADS:
+            load(t0, t1)
 
         banks = {}
         ready = {}
@@ -77,13 +85,13 @@ def tile_metalstmcell_pa_t_kernel(tc, src_x, zx, dx_w, w_x, out):
             xp = ps.tile([P, GT, 2, P], F32, name="xp", tag="xp")
             zp = ps.tile([P, GT * G * P], BF16, name="zp", tag="zp")
             for a in range(GT):
-                c, tl = divmod(j * GT + a, CH)
+                c, tl = chunk_of(j * GT + a)
                 xw = x_sb[c][:].bitcast(F32)
                 for u in range(2):
                     lo = tl * (ROW // 2) + u * P
                     nc.tensor.transpose(xp[:, a, u, :], xw[:, lo:lo + P], ident_f[:])
             for a in range(GT):
-                c, tl = divmod(j * GT + a, CH)
+                c, tl = chunk_of(j * GT + a)
                 for g in range(G):
                     lo = tl * ROW + g * Z
                     nc.tensor.transpose(zp[:, (a * G + g) * P:(a * G + g + 1) * P], z_sb[c][:, lo:lo + Z], ident_b[:])
@@ -126,15 +134,16 @@ def tile_metalstmcell_pa_t_kernel(tc, src_x, zx, dx_w, w_x, out):
                 dss.append(ds)
             dcopy[j] = dss
 
-        transposes(0)
-        transposes(1)
-        evacuate(0, False)
+        dummies(DUMMIES[0])
         dwp = ps.tile([P, GT * G * P], BF16, name="zp", tag="zp")
         for g in range(G):
             nc.tensor.transpose(dwp[:, g * H:(g + 1) * H], dw_sb[:, g * Z:(g + 1) * Z], ident_b[:])
         dwt = const.tile([P, G * H], BF16, name="dwt")
         nc.scalar.copy(out=dwt[:].bitcast(F32), in_=dwp[:, 0:G * H].bitcast(F32))
-        evacuate(1, False)
+        dummies(DUMMIES[1])
+        transposes(0)
+        evacuate(0, False)
+        dummies(DUMMIES[2])
 
         wg = const.tile([P, G * H * 4], BF16, name="wg", align_bytes=64)
         wgf = wg[:].bitcast(F32).rearrange("p (q a n u) -> p q a n u", q=2, a=GT, u=2)
@@ -150,20 +159,25 @@ def tile_metalstmcell_pa_t_kernel(tc, src_x, zx, dx_w, w_x, out):
             else:
                 nc.vector.tensor_copy(out=wgf[:, q], in_=wt[:].rearrange("p a u n -> p a n u"))
         quantise(0)
+        dummies(DUMMIES[3])
+        transposes(1)
+        evacuate(1, False)
         wc = const.tile([P, G * H], U32, name="wc", align_bytes=64)
         ws = const.tile([P, G * H], U8, name="ws", align_bytes=64)
         nc.vector.quantize_mx(out=wc[:].bitcast(FP8X4), scales=ws[:], in_=wg[:])
-        transposes(2)
+        dummies(DUMMIES[4])
         scaling_matmuls(0, 0)
         scaling_matmuls(0, 1)
         scaling_copies(0)
 
+        store_end = []
+        for n in STORE_SIZES:
+            store_end.append((store_end[-1] if store_end else 0) + n)
         obs = {}
         n_stored = 0
         for j in range(NG):
-            if j + 3 < NG:
-                transposes(j + 3)
             if j + 2 < NG:
+                transposes(j + 2)
                 evacuate(j + 2, j % 2 == 0)
             if j + 1 < NG:
                 quantise(j + 1)
@@ -187,11 +201,10 @@ def tile_metalstmcell_pa_t_kernel(tc, src_x, zx, dx_w, w_x, out):
                     obs[slot] = ob
                 nc.vector.tensor_tensor(out=obs[slot][:, tl * ROW:(tl + 1) * ROW], in0=wps[a][:],
                                         in1=dcopy[j][a][:], op=MULT)
-                s0, s1 = STORES[n_stored]
-                if t + 1 == s1:
-                    nc.sync.dma_start(out=o_v[:, s0 * ROW:s1 * ROW],
-                                      in_=obs[slot][:, (s0 - slot * ST) * ROW:(s1 - slot * ST) * ROW])
-                    late = LATE_AFTER_STORE.get(n_stored)
-                    if late is not None:
-                        load(late, 0, CH)
+                if t + 1 == store_end[n_stored]:
+                    s0 = t + 1 - STORE_SIZES[n_stored]
+                    nc.sync.dma_start(out=o_v[:, s0 * ROW:(t + 1) * ROW],
+                                      in_=obs[slot][:, (s0 - slot * ST) * ROW:(tl + 1) * ROW])
+                    for t0, t1 in LATE_LOADS.get(n_stored, []):
+                        load(t0, t1)
                     n_stored += 1

@@ -178,7 +178,7 @@ def tile_metalstmcell_pa_t_kernel(tc, src_x, zx, dx_w, w_x, out):
         for j in range(NG):
             if j + 2 < NG:
                 transposes(j + 2)
-                evacuate(j + 2, j % 2 == 0)
+                evacuate(j + 2, j % 4 == 0)
             if j + 1 < NG:
                 quantise(j + 1)
                 scaling_matmuls(j + 1, 0)

@@ -8,203 +8,207 @@ F32 = mybir.dt.float32
 U32 = mybir.dt.uint32
 U8 = mybir.dt.uint8
 FP8X4 = mybir.dt.float8_e4m3fn_x4
-MULT = mybir.AluOpType.mult
 
 P = 128
 B, IN, H, Z, G = 8192, 512, 128, 128, 4
 FLOPS = 2 * B * IN * G * H + 2 * B * G * H * Z
 ROW = 512
+WORDS = ROW // 2
 NT = B // P
 GT = 2
 NG = NT // GT
-CHUNKS = [(0, 16), (16, 24), (24, 32), (32, 48), (48, 64)]
-CHUNK_TAG = ["a", "b", "c", "d", "a"]
-EARLY_LOADS = [(2, 4), (4, 6), (6, 8), (8, 12), (12, 16), (16, 24), (24, 32), (32, 48)]
-LATE_LOADS = {1: [(48, 64)]}
-ST = 8
-STORE_SIZES = [8, 8, 8, 8, 8, 4, 4, 4, 4, 2, 2, 2, 1, 1]
-DUMMIES = [0, 0, 0, 0, 0]
+
+LOAD_PIECES = (2, 2, 2, 2, 4, 4, 8, 8, 16, 16)
+FIRST_STORES = 2
+STORE_PIECES = (8, 8, 8, 8, 8, 4, 4, 4, 4, 2, 2, 2, 1, 1)
+OUT_TILES = 8
+X_COPY_ON_SCALAR_EVERY = 4
 
 
 def tile_metalstmcell_pa_t_kernel(tc, src_x, zx, dx_w, w_x, out):
     nc = tc.nc
-    x_v = src_x.rearrange("(p t) k -> p (t k)", t=NT)
-    z_v = zx.rearrange("(p t) g z -> p (t g z)", t=NT)
-    o_v = out.rearrange("(p t) g h -> p (t g h)", t=NT)
+    x_rows = src_x.rearrange("(p t) k -> p (t k)", t=NT)
+    z_rows = zx.rearrange("(p t) g z -> p (t g z)", t=NT)
+    out_rows = out.rearrange("(p t) g h -> p (t g h)", t=NT)
 
     with ExitStack() as ctx:
         const = ctx.enter_context(tc.tile_pool(name="const", bufs=1))
-        xin = ctx.enter_context(tc.tile_pool(name="xin", bufs=1))
+        inputs = ctx.enter_context(tc.tile_pool(name="inputs", bufs=1))
         work = ctx.enter_context(tc.tile_pool(name="work", bufs=3))
-        outp = ctx.enter_context(tc.tile_pool(name="outp", bufs=4))
-        ps = ctx.enter_context(tc.psum_pool(name="ps", bufs=2))
+        results = ctx.enter_context(tc.tile_pool(name="results", bufs=4))
+        psum = ctx.enter_context(tc.psum_pool(name="psum", bufs=2))
         ctx.enter_context(tc.manual_schedule())
-
-        def dummies(n):
-            assert n == 0
 
         ident_b = const.tile([P, P], BF16, name="ident_b")
         make_identity(nc, ident_b[:])
         ident_f = const.tile([P, P], F32, name="ident_f")
         make_identity(nc, ident_f[:])
 
-        x_sb = {}
-        z_sb = {}
+        x_sb = []
+        z_sb = []
+        place = {}
+        for i, n in enumerate(LOAD_PIECES):
+            x_sb.append(inputs.tile([P, n * ROW], BF16, name="x%d" % i))
+            z_sb.append(inputs.tile([P, n * ROW], BF16, name="z%d" % i))
+            for t in range(n):
+                place[len(place)] = (i, t)
 
-        def chunk_of(t):
-            for c in range(len(CHUNKS)):
-                if CHUNKS[c][0] <= t < CHUNKS[c][1]:
-                    return c, t - CHUNKS[c][0]
-            raise ValueError("no chunk")
+        def load(i):
+            lo = sum(LOAD_PIECES[:i]) * ROW
+            hi = lo + LOAD_PIECES[i] * ROW
+            nc.sync.dma_start(out=x_sb[i][:], in_=x_rows[:, lo:hi])
+            nc.sync.dma_start(out=z_sb[i][:], in_=z_rows[:, lo:hi])
 
-        def load(t0, t1):
-            c, lo = chunk_of(t0)
-            n = CHUNKS[c][1] - CHUNKS[c][0]
-            if c not in x_sb:
-                x_sb[c] = xin.tile([P, n * ROW], BF16, name="x%s" % CHUNK_TAG[c], tag="x%s" % CHUNK_TAG[c])
-                z_sb[c] = xin.tile([P, n * ROW], BF16, name="z%s" % CHUNK_TAG[c], tag="z%s" % CHUNK_TAG[c])
-            hi = lo + t1 - t0
-            nc.sync.dma_start(out=x_sb[c][:, lo * ROW:hi * ROW], in_=x_v[:, t0 * ROW:t1 * ROW])
-            nc.sync.dma_start(out=z_sb[c][:, lo * ROW:hi * ROW], in_=z_v[:, t0 * ROW:t1 * ROW])
-
-        w_sb = const.tile([P, G * IN], BF16, name="w_sb")
         dw_sb = const.tile([P, G * Z], BF16, name="dw_sb")
+        w_sb = const.tile([P, G * IN], BF16, name="w_sb")
         nc.sync.dma_start(out=dw_sb[:].rearrange("h (g z) -> h g z", g=G), in_=dx_w.rearrange("g h z -> h g z"))
-        load(0, 2)
+        load(0)
         nc.sync.dma_start(out=w_sb[:].rearrange("h (g k) -> h g k", g=G), in_=w_x.rearrange("g h k -> h g k"))
-        for t0, t1 in EARLY_LOADS:
-            load(t0, t1)
+        for i in range(1, len(LOAD_PIECES) - 1):
+            load(i)
 
-        banks = {}
-        ready = {}
-        codes = {}
-        dcopy = {}
-        dbank = {}
+        x_bank = {}
+        z_bank = {}
+        x_pairs = {}
+        z_t = {}
+        x_mx = {}
+        d_bank = {}
+        d_sb = {}
 
-        def transposes(j):
-            xp = ps.tile([P, GT, 2, P], F32, name="xp", tag="xp")
-            zp = ps.tile([P, GT * G * P], BF16, name="zp", tag="zp")
+        def word_transposes(bank, words, first_word):
             for a in range(GT):
-                c, tl = chunk_of(j * GT + a)
-                xw = x_sb[c][:].bitcast(F32)
                 for u in range(2):
-                    lo = tl * (ROW // 2) + u * P
-                    nc.tensor.transpose(xp[:, a, u, :], xw[:, lo:lo + P], ident_f[:])
-            for a in range(GT):
-                c, tl = chunk_of(j * GT + a)
-                for g in range(G):
-                    lo = tl * ROW + g * Z
-                    nc.tensor.transpose(zp[:, (a * G + g) * P:(a * G + g + 1) * P], z_sb[c][:, lo:lo + Z], ident_b[:])
-            banks[j] = (xp, zp)
+                    lo = first_word + a * WORDS + u * P
+                    nc.tensor.transpose(bank[:, a, u, :], words[:, lo:lo + P], ident_f[:])
 
-        def evacuate(j, x_on_scalar):
-            xp, zp = banks[j]
-            xg = work.tile([P, GT * P * 4], BF16, name="xg", tag="xg", align_bytes=64)
-            dst = xg[:].bitcast(F32).rearrange("p (a b u) -> p a b u", a=GT, u=2)
-            src = xp[:].rearrange("p a u b -> p a b u")
-            if x_on_scalar:
-                nc.scalar.copy(out=dst, in_=src)
-            else:
-                nc.vector.tensor_copy(out=dst, in_=src)
-            zt = work.tile([P, GT * G * P], BF16, name="zt", tag="zt")
-            nc.scalar.copy(out=zt[:].bitcast(F32), in_=zp[:].bitcast(F32))
-            ready[j] = (xg, zt)
+        def pair_words(copy, dst, bank):
+            copy(out=dst.bitcast(F32).rearrange("p (a r u) -> p a r u", a=GT, u=2),
+                 in_=bank[:].rearrange("p a u r -> p a r u"))
+
+        def transpose_x(j):
+            i, t = place[j * GT]
+            x_bank[j] = psum.tile([P, GT, 2, P], F32, name="xp", tag="xp")
+            word_transposes(x_bank[j], x_sb[i][:].bitcast(F32), t * WORDS)
+
+        def open_z(j):
+            z_bank[j] = psum.tile([P, GT * ROW], BF16, name="zp", tag="zp")
+
+        def transpose_z(j, a, g):
+            i, t = place[j * GT + a]
+            lo = a * ROW + g * P
+            nc.tensor.transpose(z_bank[j][:, lo:lo + P], z_sb[i][:, t * ROW + g * Z:t * ROW + (g + 1) * Z],
+                                ident_b[:])
+
+        def copy_x(j):
+            x_pairs[j] = work.tile([P, GT * P * 4], BF16, name="xg", tag="xg", align_bytes=64)
+            on_scalar = j % X_COPY_ON_SCALAR_EVERY == 2
+            pair_words(nc.scalar.copy if on_scalar else nc.vector.tensor_copy, x_pairs[j][:], x_bank[j])
+
+        def copy_z(j):
+            z_t[j] = work.tile([P, GT * ROW], BF16, name="zt", tag="zt")
+            nc.scalar.copy(out=z_t[j][:].bitcast(F32), in_=z_bank[j][:].bitcast(F32))
 
         def quantise(j):
-            xg = ready[j][0]
-            xc = work.tile([P, GT * P], U32, name="xc", tag="xc", align_bytes=64)
-            xs = work.tile([P, GT * P], U8, name="xs", tag="xs", align_bytes=64)
-            nc.vector.quantize_mx(out=xc[:].bitcast(FP8X4), scales=xs[:], in_=xg[:])
-            codes[j] = (xc, xs)
+            codes = work.tile([P, GT * P], U32, name="xc", tag="xc", align_bytes=64)
+            scales = work.tile([P, GT * P], U8, name="xs", tag="xs", align_bytes=64)
+            nc.vector.quantize_mx(out=codes[:].bitcast(FP8X4), scales=scales[:], in_=x_pairs[j][:])
+            x_mx[j] = (codes, scales)
 
-        def scaling_matmuls(j, a):
-            zt = ready[j][1]
-            dp = ps.tile([P, ROW], F32, name="dp", tag="dp")
-            for g in range(G):
-                lo = (a * G + g) * P
-                nc.tensor.matmul(dp[:, g * H:(g + 1) * H], lhsT=zt[:, lo:lo + P],
-                                 rhs=dwt[:, g * H:(g + 1) * H], start=True, stop=True)
-            dbank[(j, a)] = dp
+        def open_d(j, a):
+            d_bank[(j, a)] = psum.tile([P, ROW], F32, name="dp", tag="dp")
 
-        def scaling_copies(j):
-            dss = []
+        def scaling_matmul(j, a, g):
+            lo = a * ROW + g * P
+            nc.tensor.matmul(d_bank[(j, a)][:, g * H:(g + 1) * H], lhsT=z_t[j][:, lo:lo + P],
+                             rhs=dw_t[:, g * H:(g + 1) * H], start=True, stop=True)
+
+        def copy_scalings(j):
             for a in range(GT):
-                ds = work.tile([P, ROW], F32, name="ds", tag="ds", bufs=6)
-                nc.scalar.copy(out=ds[:], in_=dbank[(j, a)][:])
-                dss.append(ds)
-            dcopy[j] = dss
+                d_sb[(j, a)] = work.tile([P, ROW], F32, name="ds", tag="ds", bufs=4)
+                nc.scalar.copy(out=d_sb[(j, a)][:], in_=d_bank[(j, a)][:])
 
-        dummies(DUMMIES[0])
-        dwp = ps.tile([P, GT * G * P], BF16, name="zp", tag="zp")
+        def projections(j):
+            codes, scales = x_mx[j]
+            banks = []
+            for a in range(GT):
+                bank = psum.tile([P, ROW], F32, name="wp", tag="wp")
+                nc.tensor.matmul_mx(out=bank[:], lhsT=codes[:, a * P:(a + 1) * P].bitcast(FP8X4),
+                                    lhsT_scale=scales[:, a * P:(a + 1) * P],
+                                    rhs=w_codes[:].bitcast(FP8X4), rhs_scale=w_scales[:], start=True, stop=True)
+                banks.append(bank)
+            return banks
+
+        dw_bank = psum.tile([P, GT * ROW], BF16, name="zp", tag="zp")
         for g in range(G):
-            nc.tensor.transpose(dwp[:, g * H:(g + 1) * H], dw_sb[:, g * Z:(g + 1) * Z], ident_b[:])
-        dwt = const.tile([P, G * H], BF16, name="dwt")
-        nc.scalar.copy(out=dwt[:].bitcast(F32), in_=dwp[:, 0:G * H].bitcast(F32))
-        dummies(DUMMIES[1])
-        transposes(0)
-        evacuate(0, False)
-        dummies(DUMMIES[2])
+            nc.tensor.transpose(dw_bank[:, g * H:(g + 1) * H], dw_sb[:, g * Z:(g + 1) * Z], ident_b[:])
+        dw_t = const.tile([P, G * H], BF16, name="dw_t")
+        nc.scalar.copy(out=dw_t[:].bitcast(F32), in_=dw_bank[:, 0:G * H].bitcast(F32))
 
-        wg = const.tile([P, G * H * 4], BF16, name="wg", align_bytes=64)
-        wgf = wg[:].bitcast(F32).rearrange("p (q a n u) -> p q a n u", q=2, a=GT, u=2)
-        wf = w_sb[:].bitcast(F32)
+        def transpose_group(j):
+            transpose_x(j)
+            open_z(j)
+            for a in range(GT):
+                for g in range(G):
+                    transpose_z(j, a, g)
+            copy_x(j)
+            copy_z(j)
+
+        transpose_group(0)
+        w_pairs = const.tile([P, G * H * 4], BF16, name="w_pairs", align_bytes=64)
         for q in range(2):
-            wt = ps.tile([P, GT, 2, P], F32, name="xp", tag="xp")
-            for a in range(GT):
-                for u in range(2):
-                    lo = (q * GT + a) * (IN // 2) + u * P
-                    nc.tensor.transpose(wt[:, a, u, :], wf[:, lo:lo + P], ident_f[:])
-            if q == 0:
-                nc.scalar.copy(out=wgf[:, q], in_=wt[:].rearrange("p a u n -> p a n u"))
-            else:
-                nc.vector.tensor_copy(out=wgf[:, q], in_=wt[:].rearrange("p a u n -> p a n u"))
+            w_bank = psum.tile([P, GT, 2, P], F32, name="xp", tag="xp")
+            word_transposes(w_bank, w_sb[:].bitcast(F32), q * GT * WORDS)
+            pair_words(nc.vector.tensor_copy if q else nc.scalar.copy,
+                       w_pairs[:, q * GT * P * 4:(q + 1) * GT * P * 4], w_bank)
         quantise(0)
-        dummies(DUMMIES[3])
-        transposes(1)
-        evacuate(1, False)
-        wc = const.tile([P, G * H], U32, name="wc", align_bytes=64)
-        ws = const.tile([P, G * H], U8, name="ws", align_bytes=64)
-        nc.vector.quantize_mx(out=wc[:].bitcast(FP8X4), scales=ws[:], in_=wg[:])
-        dummies(DUMMIES[4])
-        scaling_matmuls(0, 0)
-        scaling_matmuls(0, 1)
-        scaling_copies(0)
+        transpose_group(1)
+        w_codes = const.tile([P, G * H], U32, name="w_codes", align_bytes=64)
+        w_scales = const.tile([P, G * H], U8, name="w_scales", align_bytes=64)
+        nc.vector.quantize_mx(out=w_codes[:].bitcast(FP8X4), scales=w_scales[:], in_=w_pairs[:])
+        for a in range(GT):
+            open_d(0, a)
+            for g in range(G):
+                scaling_matmul(0, a, g)
+        copy_scalings(0)
 
-        store_end = []
-        for n in STORE_SIZES:
-            store_end.append((store_end[-1] if store_end else 0) + n)
-        obs = {}
-        n_stored = 0
+        store_ends = [sum(STORE_PIECES[:i + 1]) for i in range(len(STORE_PIECES))]
+        stored = 0
         for j in range(NG):
-            if j + 2 < NG:
-                transposes(j + 2)
-                evacuate(j + 2, j % 4 == 0)
-            if j + 1 < NG:
+            ahead = j + 2 < NG
+            following = j + 1 < NG
+            if ahead:
+                transpose_x(j + 2)
+                open_z(j + 2)
+                for g in range(G):
+                    transpose_z(j + 2, 0, g)
+                copy_x(j + 2)
+            if following:
                 quantise(j + 1)
-                scaling_matmuls(j + 1, 0)
-            xc, xs = codes[j]
-            wps = []
-            for a in range(GT):
-                wp = ps.tile([P, ROW], F32, name="wp", tag="wp")
-                nc.tensor.matmul_mx(out=wp[:], lhsT=xc[:, a * P:(a + 1) * P].bitcast(FP8X4),
-                                    lhsT_scale=xs[:, a * P:(a + 1) * P],
-                                    rhs=wc[:].bitcast(FP8X4), rhs_scale=ws[:], start=True, stop=True)
-                wps.append(wp)
-            if j + 1 < NG:
-                scaling_matmuls(j + 1, 1)
-                scaling_copies(j + 1)
+                open_d(j + 1, 0)
+            for g in range(G):
+                if ahead:
+                    transpose_z(j + 2, 1, g)
+                if following:
+                    scaling_matmul(j + 1, 0, g)
+            if ahead:
+                copy_z(j + 2)
+            w_banks = projections(j)
+            if following:
+                open_d(j + 1, 1)
+                for g in range(G):
+                    scaling_matmul(j + 1, 1, g)
+                copy_scalings(j + 1)
             for a in range(GT):
                 t = j * GT + a
-                slot, tl = divmod(t, ST)
-                if tl == 0:
-                    ob = outp.tile([P, ST * ROW], F32, name="ob", tag="ob")
-                    obs[slot] = ob
-                nc.vector.tensor_tensor(out=obs[slot][:, tl * ROW:(tl + 1) * ROW], in0=wps[a][:],
-                                        in1=dcopy[j][a][:], op=MULT)
-                if t + 1 == store_end[n_stored]:
-                    s0 = t + 1 - STORE_SIZES[n_stored]
-                    nc.sync.dma_start(out=o_v[:, s0 * ROW:(t + 1) * ROW],
-                                      in_=obs[slot][:, (s0 - slot * ST) * ROW:(tl + 1) * ROW])
-                    for t0, t1 in LATE_LOADS.get(n_stored, []):
-                        load(t0, t1)
-                    n_stored += 1
+                at = t % OUT_TILES
+                if at == 0:
+                    res = results.tile([P, OUT_TILES * ROW], F32, name="res", tag="res")
+                nc.vector.tensor_tensor(out=res[:, at * ROW:(at + 1) * ROW], in0=w_banks[a][:],
+                                        in1=d_sb[(j, a)][:], op=mybir.AluOpType.mult)
+                if t + 1 == store_ends[stored]:
+                    n = STORE_PIECES[stored]
+                    nc.sync.dma_start(out=out_rows[:, (t + 1 - n) * ROW:(t + 1) * ROW],
+                                      in_=res[:, (at + 1 - n) * ROW:(at + 1) * ROW])
+                    stored += 1
+                    if stored == FIRST_STORES:
+                        load(len(LOAD_PIECES) - 1)

@@ -165,6 +165,10 @@ def tile_metalstmcell_pa_t_kernel(tc, src_x, zx, dx_w, w_x, out):
         w_codes = const.tile([P, G * H], U32, name="w_codes", align_bytes=64)
         w_scales = const.tile([P, G * H], U8, name="w_scales", align_bytes=64)
         nc.vector.quantize_mx(out=w_codes[:].bitcast(FP8X4), scales=w_scales[:], in_=w_pairs[:])
+        open_z(2)
+        for a in range(GT):
+            for g in range(G):
+                transpose_z(2, a, g)
         for a in range(GT):
             open_d(0, a)
             for g in range(G):
@@ -176,27 +180,30 @@ def tile_metalstmcell_pa_t_kernel(tc, src_x, zx, dx_w, w_x, out):
         for j in range(NG):
             ahead = j + 2 < NG
             following = j + 1 < NG
+            further = j + 3 < NG
             if ahead:
                 transpose_x(j + 2)
-                open_z(j + 2)
-                for g in range(G):
-                    transpose_z(j + 2, 0, g)
+                copy_z(j + 2)
                 copy_x(j + 2)
             if following:
                 quantise(j + 1)
                 open_d(j + 1, 0)
+            if further:
+                open_z(j + 3)
             for g in range(G):
-                if ahead:
-                    transpose_z(j + 2, 1, g)
+                if further:
+                    transpose_z(j + 3, 0, g)
                 if following:
                     scaling_matmul(j + 1, 0, g)
-            if ahead:
-                copy_z(j + 2)
             w_banks = projections(j)
             if following:
                 open_d(j + 1, 1)
-                for g in range(G):
+            for g in range(G):
+                if following:
                     scaling_matmul(j + 1, 1, g)
+                if further:
+                    transpose_z(j + 3, 1, g)
+            if following:
                 copy_scalings(j + 1)
             for a in range(GT):
                 t = j * GT + a

from contextlib import ExitStack

import concourse.mybir as mybir
from concourse.masks import make_identity

BF16 = mybir.dt.bfloat16
F32 = mybir.dt.float32
U32 = mybir.dt.uint32
U8 = mybir.dt.uint8
FP8X4 = mybir.dt.float8_e4m3fn_x4

P = 128
B, IN, H, Z, G = 8192, 512, 128, 128, 4
FLOPS = 2 * B * IN * G * H + 2 * B * G * H * Z
ROW = 512
WORDS = ROW // 2
NT = B // P
GT = 2
NG = NT // GT

LOAD_PIECES = (2, 2, 2, 2, 4, 4, 8, 8, 16, 16)
FIRST_STORES = 2
STORE_PIECES = (8, 8, 8, 8, 8, 4, 4, 4, 4, 2, 2, 2, 1, 1)
OUT_TILES = 8
X_COPY_ON_SCALAR_EVERY = 4


def tile_metalstmcell_pa_t_kernel(tc, src_x, zx, dx_w, w_x, out):
    nc = tc.nc
    x_rows = src_x.rearrange("(p t) k -> p (t k)", t=NT)
    z_rows = zx.rearrange("(p t) g z -> p (t g z)", t=NT)
    out_rows = out.rearrange("(p t) g h -> p (t g h)", t=NT)

    with ExitStack() as ctx:
        const = ctx.enter_context(tc.tile_pool(name="const", bufs=1))
        inputs = ctx.enter_context(tc.tile_pool(name="inputs", bufs=1))
        work = ctx.enter_context(tc.tile_pool(name="work", bufs=3))
        results = ctx.enter_context(tc.tile_pool(name="results", bufs=4))
        psum = ctx.enter_context(tc.psum_pool(name="psum", bufs=2))
        ctx.enter_context(tc.manual_schedule())

        ident_b = const.tile([P, P], BF16, name="ident_b")
        make_identity(nc, ident_b[:])
        ident_f = const.tile([P, P], F32, name="ident_f")
        make_identity(nc, ident_f[:])

        x_sb = []
        z_sb = []
        place = {}
        for i, n in enumerate(LOAD_PIECES):
            x_sb.append(inputs.tile([P, n * ROW], BF16, name="x%d" % i))
            z_sb.append(inputs.tile([P, n * ROW], BF16, name="z%d" % i))
            for t in range(n):
                place[len(place)] = (i, t)

        def load(i):
            lo = sum(LOAD_PIECES[:i]) * ROW
            hi = lo + LOAD_PIECES[i] * ROW
            nc.sync.dma_start(out=x_sb[i][:], in_=x_rows[:, lo:hi])
            nc.sync.dma_start(out=z_sb[i][:], in_=z_rows[:, lo:hi])

        dw_sb = const.tile([P, G * Z], BF16, name="dw_sb")
        w_sb = const.tile([P, G * IN], BF16, name="w_sb")
        nc.sync.dma_start(out=dw_sb[:].rearrange("h (g z) -> h g z", g=G), in_=dx_w.rearrange("g h z -> h g z"))
        load(0)
        nc.sync.dma_start(out=w_sb[:].rearrange("h (g k) -> h g k", g=G), in_=w_x.rearrange("g h k -> h g k"))
        for i in range(1, len(LOAD_PIECES) - 1):
            load(i)

        x_bank = {}
        z_bank = {}
        x_pairs = {}
        z_t = {}
        x_mx = {}
        d_bank = {}
        d_sb = {}

        def word_transposes(bank, words, first_word):
            for a in range(GT):
                for u in range(2):
                    lo = first_word + a * WORDS + u * P
                    nc.tensor.transpose(bank[:, a, u, :], words[:, lo:lo + P], ident_f[:])

        def pair_words(copy, dst, bank):
            copy(out=dst.bitcast(F32).rearrange("p (a r u) -> p a r u", a=GT, u=2),
                 in_=bank[:].rearrange("p a u r -> p a r u"))

        def transpose_x(j):
            i, t = place[j * GT]
            x_bank[j] = psum.tile([P, GT, 2, P], F32, name="xp", tag="xp")
            word_transposes(x_bank[j], x_sb[i][:].bitcast(F32), t * WORDS)

        def open_z(j):
            z_bank[j] = psum.tile([P, GT * ROW], BF16, name="zp", tag="zp")

        def transpose_z(j, a, g):
            i, t = place[j * GT + a]
            lo = a * ROW + g * P
            nc.tensor.transpose(z_bank[j][:, lo:lo + P], z_sb[i][:, t * ROW + g * Z:t * ROW + (g + 1) * Z],
                                ident_b[:])

        def copy_x(j):
            x_pairs[j] = work.tile([P, GT * P * 4], BF16, name="xg", tag="xg", align_bytes=64)
            on_scalar = j % X_COPY_ON_SCALAR_EVERY == 2
            pair_words(nc.scalar.copy if on_scalar else nc.vector.tensor_copy, x_pairs[j][:], x_bank[j])

        def copy_z(j):
            z_t[j] = work.tile([P, GT * ROW], BF16, name="zt", tag="zt")
            nc.scalar.copy(out=z_t[j][:].bitcast(F32), in_=z_bank[j][:].bitcast(F32))

        def quantise(j):
            codes = work.tile([P, GT * P], U32, name="xc", tag="xc", align_bytes=64)
            scales = work.tile([P, GT * P], U8, name="xs", tag="xs", align_bytes=64)
            nc.vector.quantize_mx(out=codes[:].bitcast(FP8X4), scales=scales[:], in_=x_pairs[j][:])
            x_mx[j] = (codes, scales)

        def open_d(j, a):
            d_bank[(j, a)] = psum.tile([P, ROW], F32, name="dp", tag="dp")

        def scaling_matmul(j, a, g):
            lo = a * ROW + g * P
            nc.tensor.matmul(d_bank[(j, a)][:, g * H:(g + 1) * H], lhsT=z_t[j][:, lo:lo + P],
                             rhs=dw_t[:, g * H:(g + 1) * H], start=True, stop=True)

        def copy_scalings(j):
            for a in range(GT):
                d_sb[(j, a)] = work.tile([P, ROW], F32, name="ds", tag="ds", bufs=4)
                nc.scalar.copy(out=d_sb[(j, a)][:], in_=d_bank[(j, a)][:])

        def projections(j):
            codes, scales = x_mx[j]
            banks = []
            for a in range(GT):
                bank = psum.tile([P, ROW], F32, name="wp", tag="wp")
                nc.tensor.matmul_mx(out=bank[:], lhsT=codes[:, a * P:(a + 1) * P].bitcast(FP8X4),
                                    lhsT_scale=scales[:, a * P:(a + 1) * P],
                                    rhs=w_codes[:].bitcast(FP8X4), rhs_scale=w_scales[:], start=True, stop=True)
                banks.append(bank)
            return banks

        dw_bank = psum.tile([P, GT * ROW], BF16, name="zp", tag="zp")
        for g in range(G):
            nc.tensor.transpose(dw_bank[:, g * H:(g + 1) * H], dw_sb[:, g * Z:(g + 1) * Z], ident_b[:])
        dw_t = const.tile([P, G * H], BF16, name="dw_t")
        nc.scalar.copy(out=dw_t[:].bitcast(F32), in_=dw_bank[:, 0:G * H].bitcast(F32))

        def transpose_group(j):
            transpose_x(j)
            open_z(j)
            for a in range(GT):
                for g in range(G):
                    transpose_z(j, a, g)
            copy_x(j)
            copy_z(j)

        transpose_group(0)
        w_pairs = const.tile([P, G * H * 4], BF16, name="w_pairs", align_bytes=64)
        for q in range(2):
            w_bank = psum.tile([P, GT, 2, P], F32, name="xp", tag="xp")
            word_transposes(w_bank, w_sb[:].bitcast(F32), q * GT * WORDS)
            pair_words(nc.vector.tensor_copy if q else nc.scalar.copy,
                       w_pairs[:, q * GT * P * 4:(q + 1) * GT * P * 4], w_bank)
        quantise(0)
        transpose_group(1)
        w_codes = const.tile([P, G * H], U32, name="w_codes", align_bytes=64)
        w_scales = const.tile([P, G * H], U8, name="w_scales", align_bytes=64)
        nc.vector.quantize_mx(out=w_codes[:].bitcast(FP8X4), scales=w_scales[:], in_=w_pairs[:])
        open_z(2)
        for a in range(GT):
            for g in range(G):
                transpose_z(2, a, g)
        for a in range(GT):
            open_d(0, a)
            for g in range(G):
                scaling_matmul(0, a, g)
        copy_scalings(0)

        store_ends = [sum(STORE_PIECES[:i + 1]) for i in range(len(STORE_PIECES))]
        stored = 0
        for j in range(NG):
            ahead = j + 2 < NG
            following = j + 1 < NG
            further = j + 3 < NG
            if ahead:
                transpose_x(j + 2)
                copy_z(j + 2)
                copy_x(j + 2)
            if following:
                quantise(j + 1)
                open_d(j + 1, 0)
            if further:
                open_z(j + 3)
            for g in range(G):
                if further:
                    transpose_z(j + 3, 0, g)
                if following:
                    scaling_matmul(j + 1, 0, g)
            w_banks = projections(j)
            if following:
                open_d(j + 1, 1)
            for g in range(G):
                if following:
                    scaling_matmul(j + 1, 1, g)
                if further:
                    transpose_z(j + 3, 1, g)
            if following:
                copy_scalings(j + 1)
            for a in range(GT):
                t = j * GT + a
                at = t % OUT_TILES
                if at == 0:
                    res = results.tile([P, OUT_TILES * ROW], F32, name="res", tag="res")
                nc.vector.tensor_tensor(out=res[:, at * ROW:(at + 1) * ROW], in0=w_banks[a][:],
                                        in1=d_sb[(j, a)][:], op=mybir.AluOpType.mult)
                if t + 1 == store_ends[stored]:
                    n = STORE_PIECES[stored]
                    nc.sync.dma_start(out=out_rows[:, (t + 1 - n) * ROW:(t + 1) * ROW],
                                      in_=res[:, (at + 1 - n) * ROW:(at + 1) * ROW])
                    stored += 1
                    if stored == FIRST_STORES:
                        load(len(LOAD_PIECES) - 1)
